import numpy as np
import ml_dtypes

BF16 = ml_dtypes.bfloat16


def bf(x):
    return np.asarray(x, np.float32).astype(BF16)


def f32(x):
    return np.asarray(x, np.float32)


def f64(x):
    return np.asarray(x).astype(np.float64)


def striped(idx):
    return np.tile(idx.reshape(-1, 16).T, (8, 1))


S, D, N, L = 256, 128, 256, 256


def setup_inputs():
    return {"table": bf(np.random.standard_normal((S, D))), "w": bf(1.8 * np.random.standard_normal((D, D)) / np.sqrt(D)), "delta": bf(0.9 * np.random.standard_normal((D, D)) / np.sqrt(D)), "b_q": f32(0.2 * np.random.standard_normal((D, 1))), "kv": bf(np.random.standard_normal((D, L))), "b_v": f32(0.1 * np.random.standard_normal((D, 1))), "offs": striped(np.random.permutation(S)[:N])}


def reference(table, w, delta, b_q, kv, b_v, offs):
    idx = offs[:16].T.reshape(-1)
    xq = f64(table)[idx].T
    q = f64(w).T @ xq + f64(delta).T @ xq + f64(b_q)
    sc = q.T @ f64(kv) / np.sqrt(D)
    e = np.exp(sc - sc.max(axis=1, keepdims=True))
    a = e / e.sum(axis=1, keepdims=True)
    return f64(kv) @ a.T + f64(b_v)

@@ -1,0 +1,99 @@
+import math
+
+import concourse.mybir as mybir
+from concourse.masks import make_identity
+
+BF16, F32, U16 = mybir.dt.bfloat16, mybir.dt.float32, mybir.dt.uint16
+EXP = mybir.ActivationFunctionType.Exp
+X = mybir.AxisListType.X
+
+P = 128
+S = 256
+N = 256
+L = 256
+SCALE = 1.0 / math.sqrt(P)
+
+FLOPS = 2 * (2 * P * P * N) + 2 * (2 * P * N * L)
+
+
+def tile_multiloramultiheadselfattenion_kernel(tc, table, w, delta, b_q, kv, b_v, offs, out):
+    nc = tc.nc
+    with (
+        tc.tile_pool(name="held", bufs=1) as held,
+        tc.tile_pool(name="work", bufs=2) as work,
+        tc.psum_pool(name="flip", bufs=2) as flip,
+        tc.psum_pool(name="proj", bufs=1) as proj,
+        tc.psum_pool(name="attn", bufs=2) as attn,
+    ):
+        offsets = held.tile([P, N // 16], U16, name="offsets")
+        nc.sync.dma_start(offsets[:], offs)
+        table_rows = held.tile([P, S], BF16, name="table_rows")
+        for b in range(S // P):
+            nc.sync.dma_start(table_rows[:, b * P : (b + 1) * P], table[b * P : (b + 1) * P, :])
+        w_sb = held.tile([P, P], BF16, name="w_sb")
+        nc.scalar.dma_start(w_sb[:], w)
+        delta_sb = held.tile([P, P], BF16, name="delta_sb")
+        nc.scalar.dma_start(delta_sb[:], delta)
+        kv_sb = held.tile([P, L], BF16, name="kv_sb")
+        nc.scalar.dma_start(kv_sb[:], kv)
+        bq_sb = held.tile([P, 1], F32, name="bq_sb")
+        nc.sync.dma_start(bq_sb[:], b_q)
+        bv_sb = held.tile([P, 1], F32, name="bv_sb")
+        nc.sync.dma_start(bv_sb[:], b_v)
+
+        identity = held.tile([P, P], BF16, name="identity")
+        make_identity(nc, identity[:])
+
+        table_t_ps = flip.tile([P, S], BF16, name="table_t_ps", tag="flip")
+        for b in range(S // P):
+            nc.tensor.transpose(table_t_ps[:, b * P : (b + 1) * P], table_rows[:, b * P : (b + 1) * P], identity[:])
+        table_t = held.tile([P, S], BF16, name="table_t")
+        nc.vector.tensor_copy(table_t[:], table_t_ps[:])
+
+        kv_t_ps = flip.tile([P, L], BF16, name="kv_t_ps", tag="flip")
+        for b in range(L // P):
+            nc.tensor.transpose(kv_t_ps[:, b * P : (b + 1) * P], kv_sb[:, b * P : (b + 1) * P], identity[:])
+        kv_t = held.tile([P, L], BF16, name="kv_t")
+        nc.vector.tensor_copy(kv_t[:], kv_t_ps[:])
+
+        q_ps = proj.tile([P, N], F32, name="q_ps")
+        nc.tensor.matmul(q_ps[:], w_sb[:], table_t[:].indirect(offsets[:]), start=True, stop=False)
+        nc.tensor.matmul(q_ps[:], delta_sb[:], table_t[:].indirect(offsets[:]), start=False, stop=True)
+        q_bf = held.tile([P, N], BF16, name="q_bf")
+        nc.vector.tensor_scalar_add(q_bf[:], q_ps[:], bq_sb[:, 0:1])
+
+        for jb in range(N // P):
+            queries = slice(jb * P, (jb + 1) * P)
+            sc_ps = attn.tile([P, L], F32, name="sc_ps")
+            nc.tensor.matmul(sc_ps[:], q_bf[:, queries], kv_sb[:], start=True, stop=True)
+
+            neg_max = work.tile([P, 1], F32, name="neg_max")
+            nc.vector.reduce_max(neg_max[:], sc_ps[:], axis=X, negate=True)
+            shift = work.tile([P, 1], F32, name="shift")
+            nc.vector.tensor_scalar_mul(shift[:], neg_max[:], SCALE)
+            e = work.tile([P, L], F32, name="e")
+            e_sum = work.tile([P, 1], F32, name="e_sum")
+            nc.scalar.activation(e[:], sc_ps[:], EXP, bias=shift[:, 0:1], scale=SCALE, accum_out=e_sum[:])
+            r_sum = work.tile([P, 1], F32, name="r_sum")
+            nc.vector.reciprocal(r_sum[:], e_sum[:])
+            a = work.tile([P, L], BF16, name="a")
+            nc.vector.tensor_scalar_mul(a[:], e[:], r_sum[:, 0:1])
+
+            a_t_ps = flip.tile([P, L], BF16, name="a_t_ps", tag="flip")
+            for b in range(L // P):
+                nc.tensor.transpose(a_t_ps[:, b * P : (b + 1) * P], a[:, b * P : (b + 1) * P], identity[:])
+            a_t = work.tile([P, L], BF16, name="a_t")
+            nc.vector.tensor_copy(a_t[:], a_t_ps[:])
+
+            o_ps = attn.tile([P, P], F32, name="o_ps")
+            for b in range(L // P):
+                nc.tensor.matmul(
+                    o_ps[:],
+                    kv_t[:, b * P : (b + 1) * P],
+                    a_t[:, b * P : (b + 1) * P],
+                    start=(b == 0),
+                    stop=(b == L // P - 1),
+                )
+            o = work.tile([P, P], F32, name="o")
+            nc.vector.tensor_scalar_add(o[:], o_ps[:], bv_sb[:, 0:1])
+            nc.sync.dma_start(out[:, queries], o[:])

@@ -12,6 +12,7 @@ S = 256
 N = 256
 L = 256
 SCALE = 1.0 / math.sqrt(P)
+WARM_UP = 6
 
 FLOPS = 2 * (2 * P * P * N) + 2 * (2 * P * N * L)
 
@@ -24,7 +25,14 @@ def tile_multiloramultiheadselfattenion_kernel(tc, table, w, delta, b_q, kv, b_v
         tc.psum_pool(name="flip", bufs=2) as flip,
         tc.psum_pool(name="proj", bufs=1) as proj,
         tc.psum_pool(name="attn", bufs=2) as attn,
+        tc.psum_pool(name="idle", bufs=1) as idle,
     ):
+        warm_in = held.tile([P, 512], BF16, name="warm_in")
+        nc.vector.memset(warm_in[:], 0.0)
+        warm_ps = idle.tile([P, 512], F32, name="warm_ps")
+        for _ in range(WARM_UP):
+            nc.tensor.matmul(warm_ps[:], warm_in[:, 0:P], warm_in[:], start=True, stop=True)
+
         offsets = held.tile([P, N // 16], U16, name="offsets")
         nc.sync.dma_start(offsets[:], offs)
         table_rows = held.tile([P, S], BF16, name="table_rows")

@@ -12,96 +12,83 @@ S = 256
 N = 256
 L = 256
 SCALE = 1.0 / math.sqrt(P)
-WARM_UP = 6
 
 FLOPS = 2 * (2 * P * P * N) + 2 * (2 * P * N * L)
 
 
 def tile_multiloramultiheadselfattenion_kernel(tc, table, w, delta, b_q, kv, b_v, offs, out):
     nc = tc.nc
+    blocks = range(N // P)
+    halves = range(L // P)
     with (
         tc.tile_pool(name="held", bufs=1) as held,
-        tc.tile_pool(name="work", bufs=2) as work,
-        tc.psum_pool(name="flip", bufs=2) as flip,
-        tc.psum_pool(name="proj", bufs=1) as proj,
-        tc.psum_pool(name="attn", bufs=2) as attn,
-        tc.psum_pool(name="idle", bufs=1) as idle,
+        tc.psum_pool(name="psum", bufs=1) as psum,
     ):
-        warm_in = held.tile([P, 512], BF16, name="warm_in")
-        nc.vector.memset(warm_in[:], 0.0)
-        warm_ps = idle.tile([P, 512], F32, name="warm_ps")
-        for _ in range(WARM_UP):
-            nc.tensor.matmul(warm_ps[:], warm_in[:, 0:P], warm_in[:], start=True, stop=True)
-
+        table_rows = held.tile([P, S], BF16, name="table_rows")
+        nc.sync.dma_start(table_rows[:, 0:P], table[0:P, :])
+        nc.scalar.dma_start(table_rows[:, P : 2 * P], table[P : 2 * P, :])
         offsets = held.tile([P, N // 16], U16, name="offsets")
         nc.sync.dma_start(offsets[:], offs)
-        table_rows = held.tile([P, S], BF16, name="table_rows")
-        for b in range(S // P):
-            nc.sync.dma_start(table_rows[:, b * P : (b + 1) * P], table[b * P : (b + 1) * P, :])
         w_sb = held.tile([P, P], BF16, name="w_sb")
         nc.scalar.dma_start(w_sb[:], w)
         delta_sb = held.tile([P, P], BF16, name="delta_sb")
-        nc.scalar.dma_start(delta_sb[:], delta)
+        nc.sync.dma_start(delta_sb[:], delta)
         kv_sb = held.tile([P, L], BF16, name="kv_sb")
         nc.scalar.dma_start(kv_sb[:], kv)
         bq_sb = held.tile([P, 1], F32, name="bq_sb")
         nc.sync.dma_start(bq_sb[:], b_q)
         bv_sb = held.tile([P, 1], F32, name="bv_sb")
-        nc.sync.dma_start(bv_sb[:], b_v)
+        nc.scalar.dma_start(bv_sb[:], b_v)
 
         identity = held.tile([P, P], BF16, name="identity")
         make_identity(nc, identity[:])
 
-        table_t_ps = flip.tile([P, S], BF16, name="table_t_ps", tag="flip")
-        for b in range(S // P):
-            nc.tensor.transpose(table_t_ps[:, b * P : (b + 1) * P], table_rows[:, b * P : (b + 1) * P], identity[:])
         table_t = held.tile([P, S], BF16, name="table_t")
-        nc.vector.tensor_copy(table_t[:], table_t_ps[:])
+        for b in range(S // P):
+            table_t_ps = psum.tile([P, P], BF16, name=f"table_t_ps{b}", tag=f"flip{b}")
+            nc.tensor.transpose(table_t_ps[:], table_rows[:, b * P : (b + 1) * P], identity[:])
+            nc.vector.tensor_copy(table_t[:, b * P : (b + 1) * P], table_t_ps[:])
 
-        kv_t_ps = flip.tile([P, L], BF16, name="kv_t_ps", tag="flip")
-        for b in range(L // P):
-            nc.tensor.transpose(kv_t_ps[:, b * P : (b + 1) * P], kv_sb[:, b * P : (b + 1) * P], identity[:])
+        kv_t_ps = psum.tile([P, L], BF16, name="kv_t_ps", tag="flip2")
+        for h in halves:
+            nc.tensor.transpose(kv_t_ps[:, h * P : (h + 1) * P], kv_sb[:, h * P : (h + 1) * P], identity[:])
         kv_t = held.tile([P, L], BF16, name="kv_t")
         nc.vector.tensor_copy(kv_t[:], kv_t_ps[:])
 
-        q_ps = proj.tile([P, N], F32, name="q_ps")
-        nc.tensor.matmul(q_ps[:], w_sb[:], table_t[:].indirect(offsets[:]), start=True, stop=False)
-        nc.tensor.matmul(q_ps[:], delta_sb[:], table_t[:].indirect(offsets[:]), start=False, stop=True)
-        q_bf = held.tile([P, N], BF16, name="q_bf")
-        nc.vector.tensor_scalar_add(q_bf[:], q_ps[:], bq_sb[:, 0:1])
+        q_ps = [psum.tile([P, P], F32, name=f"q_ps{jb}", tag=f"q_o{jb}") for jb in blocks]
+        q_bf = [held.tile([P, P], BF16, name=f"q_bf{jb}") for jb in blocks]
+        for jb in blocks:
+            piece = offsets[:, jb * (P // 16) : (jb + 1) * (P // 16)]
+            nc.tensor.matmul(q_ps[jb][:], w_sb[:], table_t[:].indirect(piece), start=True, stop=False)
+            nc.tensor.matmul(q_ps[jb][:], delta_sb[:], table_t[:].indirect(piece), start=False, stop=True)
+        for jb in blocks:
+            nc.vector.tensor_scalar_add(q_bf[jb][:], q_ps[jb][:], bq_sb[:, 0:1])
 
-        for jb in range(N // P):
-            queries = slice(jb * P, (jb + 1) * P)
-            sc_ps = attn.tile([P, L], F32, name="sc_ps")
-            nc.tensor.matmul(sc_ps[:], q_bf[:, queries], kv_sb[:], start=True, stop=True)
+        sc_ps = [psum.tile([P, L], F32, name=f"sc_ps{jb}") for jb in blocks]
+        for jb in blocks:
+            nc.tensor.matmul(sc_ps[jb][:], q_bf[jb][:], kv_sb[:], start=True, stop=True)
 
-            neg_max = work.tile([P, 1], F32, name="neg_max")
-            nc.vector.reduce_max(neg_max[:], sc_ps[:], axis=X, negate=True)
-            shift = work.tile([P, 1], F32, name="shift")
-            nc.vector.tensor_scalar_mul(shift[:], neg_max[:], SCALE)
-            e = work.tile([P, L], F32, name="e")
-            e_sum = work.tile([P, 1], F32, name="e_sum")
-            nc.scalar.activation(e[:], sc_ps[:], EXP, bias=shift[:, 0:1], scale=SCALE, accum_out=e_sum[:])
-            r_sum = work.tile([P, 1], F32, name="r_sum")
-            nc.vector.reciprocal(r_sum[:], e_sum[:])
-            a = work.tile([P, L], BF16, name="a")
-            nc.vector.tensor_scalar_mul(a[:], e[:], r_sum[:, 0:1])
-
-            a_t_ps = flip.tile([P, L], BF16, name="a_t_ps", tag="flip")
-            for b in range(L // P):
-                nc.tensor.transpose(a_t_ps[:, b * P : (b + 1) * P], a[:, b * P : (b + 1) * P], identity[:])
-            a_t = work.tile([P, L], BF16, name="a_t")
-            nc.vector.tensor_copy(a_t[:], a_t_ps[:])
-
-            o_ps = attn.tile([P, P], F32, name="o_ps")
-            for b in range(L // P):
-                nc.tensor.matmul(
-                    o_ps[:],
-                    kv_t[:, b * P : (b + 1) * P],
-                    a_t[:, b * P : (b + 1) * P],
-                    start=(b == 0),
-                    stop=(b == L // P - 1),
-                )
-            o = work.tile([P, P], F32, name="o")
-            nc.vector.tensor_scalar_add(o[:], o_ps[:], bv_sb[:, 0:1])
-            nc.sync.dma_start(out[:, queries], o[:])
+        neg_max = [held.tile([P, 1], F32, name=f"neg_max{jb}") for jb in blocks]
+        shift = [held.tile([P, 1], F32, name=f"shift{jb}") for jb in blocks]
+        e = [held.tile([P, L], F32, name=f"e{jb}") for jb in blocks]
+        e_sum = [held.tile([P, 1], F32, name=f"e_sum{jb}") for jb in blocks]
+        r_sum = [held.tile([P, 1], F32, name=f"r_sum{jb}") for jb in blocks]
+        a = [held.tile([P, L], BF16, name=f"a{jb}") for jb in blocks]
+        for jb in blocks:
+            nc.vector.reduce_max(neg_max[jb][:], sc_ps[jb][:], axis=X, negate=True)
+            nc.vector.tensor_scalar_mul(shift[jb][:], neg_max[jb][:], SCALE)
+            nc.scalar.activation(e[jb][:], sc_ps[jb][:], EXP, bias=shift[jb][:, 0:1], scale=SCALE, accum_out=e_sum[jb][:])
+        a_t = [held.tile([P, L], BF16, name=f"a_t{jb}") for jb in blocks]
+        o_ps = [psum.tile([P, P], F32, name=f"o_ps{jb}", tag=f"q_o{jb}") for jb in blocks]
+        o = [held.tile([P, P], F32, name=f"o{jb}") for jb in blocks]
+        for jb in blocks:
+            nc.vector.reciprocal(r_sum[jb][:], e_sum[jb][:])
+            for h in halves:
+                keys = slice(h * P, (h + 1) * P)
+                nc.vector.tensor_scalar_mul(a[jb][:, keys], e[jb][:, keys], r_sum[jb][:, 0:1])
+                a_t_ps = psum.tile([P, P], BF16, name=f"a_t_ps{jb}{h}", tag=f"flip{2 * jb + h}")
+                nc.tensor.transpose(a_t_ps[:], a[jb][:, keys], identity[:])
+                nc.vector.tensor_copy(a_t[jb][:, keys], a_t_ps[:])
+                nc.tensor.matmul(o_ps[jb][:], kv_t[:, keys], a_t[jb][:, keys], start=(h == 0), stop=(h == L // P - 1))
+            nc.vector.tensor_scalar_add(o[jb][:], o_ps[jb][:], bv_sb[:, 0:1])
+            nc.sync.dma_start(out[:, jb * P : (jb + 1) * P], o[jb][:])

@@ -5,7 +5,7 @@ from concourse.masks import make_identity
 
 BF16, F32, U16 = mybir.dt.bfloat16, mybir.dt.float32, mybir.dt.uint16
 EXP = mybir.ActivationFunctionType.Exp
-X = mybir.AxisListType.X
+MULT, MIN = mybir.AluOpType.mult, mybir.AluOpType.min
 
 P = 128
 S = 256
@@ -68,16 +68,15 @@ def tile_multiloramultiheadselfattenion_kernel(tc, table, w, delta, b_q, kv, b_v
         for jb in blocks:
             nc.tensor.matmul(sc_ps[jb][:], q_bf[jb][:], kv_sb[:], start=True, stop=True)
 
-        neg_max = [held.tile([P, 1], F32, name=f"neg_max{jb}") for jb in blocks]
+        neg_sc = [held.tile([P, L], F32, name=f"neg_sc{jb}") for jb in blocks]
         shift = [held.tile([P, 1], F32, name=f"shift{jb}") for jb in blocks]
         e = [held.tile([P, L], F32, name=f"e{jb}") for jb in blocks]
         e_sum = [held.tile([P, 1], F32, name=f"e_sum{jb}") for jb in blocks]
         r_sum = [held.tile([P, 1], F32, name=f"r_sum{jb}") for jb in blocks]
         a = [held.tile([P, L], BF16, name=f"a{jb}") for jb in blocks]
         for jb in blocks:
-            nc.vector.reduce_max(neg_max[jb][:], sc_ps[jb][:], axis=X, negate=True)
-            nc.vector.tensor_scalar_mul(shift[jb][:], neg_max[jb][:], SCALE)
-            nc.scalar.activation(e[jb][:], sc_ps[jb][:], EXP, bias=shift[jb][:, 0:1], scale=SCALE, accum_out=e_sum[jb][:])
+            nc.vector.tensor_scalar(neg_sc[jb][:], sc_ps[jb][:], -SCALE, None, op0=MULT, op1=MIN, accum_out=shift[jb][:])
+            nc.scalar.activation(e[jb][:], neg_sc[jb][:], EXP, bias=shift[jb][:, 0:1], scale=-1.0, accum_out=e_sum[jb][:])
         a_t = [held.tile([P, L], BF16, name=f"a_t{jb}") for jb in blocks]
         o_ps = [psum.tile([P, P], F32, name=f"o_ps{jb}", tag=f"q_o{jb}") for jb in blocks]
         o = [held.tile([P, P], F32, name=f"o{jb}") for jb in blocks]

@@ -49,12 +49,6 @@ def tile_multiloramultiheadselfattenion_kernel(tc, table, w, delta, b_q, kv, b_v
             nc.tensor.transpose(table_t_ps[:], table_rows[:, b * P : (b + 1) * P], identity[:])
             nc.vector.tensor_copy(table_t[:, b * P : (b + 1) * P], table_t_ps[:])
 
-        kv_t_ps = psum.tile([P, L], BF16, name="kv_t_ps", tag="flip2")
-        for h in halves:
-            nc.tensor.transpose(kv_t_ps[:, h * P : (h + 1) * P], kv_sb[:, h * P : (h + 1) * P], identity[:])
-        kv_t = held.tile([P, L], BF16, name="kv_t")
-        nc.vector.tensor_copy(kv_t[:], kv_t_ps[:])
-
         q_ps = [psum.tile([P, P], F32, name=f"q_ps{jb}", tag=f"q_o{jb}") for jb in blocks]
         q_bf = [held.tile([P, P], BF16, name=f"q_bf{jb}") for jb in blocks]
         for jb in blocks:
@@ -77,6 +71,13 @@ def tile_multiloramultiheadselfattenion_kernel(tc, table, w, delta, b_q, kv, b_v
         for jb in blocks:
             nc.vector.tensor_scalar(neg_sc[jb][:], sc_ps[jb][:], -SCALE, None, op0=MULT, op1=MIN, accum_out=shift[jb][:])
             nc.scalar.activation(e[jb][:], neg_sc[jb][:], EXP, bias=shift[jb][:, 0:1], scale=-1.0, accum_out=e_sum[jb][:])
+
+        kv_t_ps = psum.tile([P, L], BF16, name="kv_t_ps", tag="flip2")
+        for h in halves:
+            nc.tensor.transpose(kv_t_ps[:, h * P : (h + 1) * P], kv_sb[:, h * P : (h + 1) * P], identity[:])
+        kv_t = held.tile([P, L], BF16, name="kv_t")
+        nc.scalar.copy(kv_t[:], kv_t_ps[:])
+
         a_t = [held.tile([P, L], BF16, name=f"a_t{jb}") for jb in blocks]
         o_ps = [psum.tile([P, P], F32, name=f"o_ps{jb}", tag=f"q_o{jb}") for jb in blocks]
         o = [held.tile([P, P], F32, name=f"o{jb}") for jb in blocks]

@@ -27,6 +27,8 @@ def tile_multiloramultiheadselfattenion_kernel(tc, table, w, delta, b_q, kv, b_v
         table_rows = held.tile([P, S], BF16, name="table_rows")
         nc.sync.dma_start(table_rows[:, 0:P], table[0:P, :])
         nc.scalar.dma_start(table_rows[:, P : 2 * P], table[P : 2 * P, :])
+        bq_sb = held.tile([P, 1], F32, name="bq_sb")
+        nc.sync.dma_start(bq_sb[:], b_q)
         offsets = held.tile([P, N // 16], U16, name="offsets")
         nc.sync.dma_start(offsets[:], offs)
         w_sb = held.tile([P, P], BF16, name="w_sb")
@@ -35,8 +37,6 @@ def tile_multiloramultiheadselfattenion_kernel(tc, table, w, delta, b_q, kv, b_v
         nc.sync.dma_start(delta_sb[:], delta)
         kv_sb = held.tile([P, L], BF16, name="kv_sb")
         nc.scalar.dma_start(kv_sb[:], kv)
-        bq_sb = held.tile([P, 1], F32, name="bq_sb")
-        nc.sync.dma_start(bq_sb[:], b_q)
         bv_sb = held.tile([P, 1], F32, name="bv_sb")
         nc.scalar.dma_start(bv_sb[:], b_v)
 
@@ -48,6 +48,12 @@ def tile_multiloramultiheadselfattenion_kernel(tc, table, w, delta, b_q, kv, b_v
             table_t_ps = psum.tile([P, P], BF16, name=f"table_t_ps{b}", tag=f"flip{b}")
             nc.tensor.transpose(table_t_ps[:], table_rows[:, b * P : (b + 1) * P], identity[:])
             nc.vector.tensor_copy(table_t[:, b * P : (b + 1) * P], table_t_ps[:])
+
+        kv_t_ps = psum.tile([P, L], BF16, name="kv_t_ps", tag="flip2")
+        for h in halves:
+            nc.tensor.transpose(kv_t_ps[:, h * P : (h + 1) * P], kv_sb[:, h * P : (h + 1) * P], identity[:])
+        kv_t = held.tile([P, L], BF16, name="kv_t")
+        nc.vector.tensor_copy(kv_t[:], kv_t_ps[:])
 
         q_ps = [psum.tile([P, P], F32, name=f"q_ps{jb}", tag=f"q_o{jb}") for jb in blocks]
         q_bf = [held.tile([P, P], BF16, name=f"q_bf{jb}") for jb in blocks]
@@ -71,13 +77,6 @@ def tile_multiloramultiheadselfattenion_kernel(tc, table, w, delta, b_q, kv, b_v
         for jb in blocks:
             nc.vector.tensor_scalar(neg_sc[jb][:], sc_ps[jb][:], -SCALE, None, op0=MULT, op1=MIN, accum_out=shift[jb][:])
             nc.scalar.activation(e[jb][:], neg_sc[jb][:], EXP, bias=shift[jb][:, 0:1], scale=-1.0, accum_out=e_sum[jb][:])
-
-        kv_t_ps = psum.tile([P, L], BF16, name="kv_t_ps", tag="flip2")
-        for h in halves:
-            nc.tensor.transpose(kv_t_ps[:, h * P : (h + 1) * P], kv_sb[:, h * P : (h + 1) * P], identity[:])
-        kv_t = held.tile([P, L], BF16, name="kv_t")
-        nc.scalar.copy(kv_t[:], kv_t_ps[:])
-
         a_t = [held.tile([P, L], BF16, name=f"a_t{jb}") for jb in blocks]
         o_ps = [psum.tile([P, P], F32, name=f"o_ps{jb}", tag=f"q_o{jb}") for jb in blocks]
         o = [held.tile([P, P], F32, name=f"o{jb}") for jb in blocks]

@@ -27,16 +27,16 @@ def tile_multiloramultiheadselfattenion_kernel(tc, table, w, delta, b_q, kv, b_v
         table_rows = held.tile([P, S], BF16, name="table_rows")
         nc.sync.dma_start(table_rows[:, 0:P], table[0:P, :])
         nc.scalar.dma_start(table_rows[:, P : 2 * P], table[P : 2 * P, :])
-        bq_sb = held.tile([P, 1], F32, name="bq_sb")
-        nc.sync.dma_start(bq_sb[:], b_q)
         offsets = held.tile([P, N // 16], U16, name="offsets")
         nc.sync.dma_start(offsets[:], offs)
-        w_sb = held.tile([P, P], BF16, name="w_sb")
-        nc.scalar.dma_start(w_sb[:], w)
         delta_sb = held.tile([P, P], BF16, name="delta_sb")
-        nc.sync.dma_start(delta_sb[:], delta)
+        nc.scalar.dma_start(delta_sb[:], delta)
+        w_sb = held.tile([P, P], BF16, name="w_sb")
+        nc.sync.dma_start(w_sb[:], w)
+        bq_sb = held.tile([P, 1], F32, name="bq_sb")
+        nc.scalar.dma_start(bq_sb[:], b_q)
         kv_sb = held.tile([P, L], BF16, name="kv_sb")
-        nc.scalar.dma_start(kv_sb[:], kv)
+        nc.sync.dma_start(kv_sb[:], kv)
         bv_sb = held.tile([P, 1], F32, name="bv_sb")
         nc.scalar.dma_start(bv_sb[:], b_v)
 

@@ -43,6 +43,11 @@ def tile_multiloramultiheadselfattenion_kernel(tc, table, w, delta, b_q, kv, b_v
         identity = held.tile([P, P], BF16, name="identity")
         make_identity(nc, identity[:])
 
+        scrap = held.tile([P, 1], F32, name="scrap")
+        nc.vector.memset(scrap[:], 0.0)
+        scrap_exp = held.tile([P, 1], F32, name="scrap_exp")
+        nc.scalar.activation(scrap_exp[:], scrap[:], EXP)
+
         table_t = held.tile([P, S], BF16, name="table_t")
         for b in range(S // P):
             table_t_ps = psum.tile([P, P], BF16, name=f"table_t_ps{b}", tag=f"flip{b}")
@@ -64,19 +69,22 @@ def tile_multiloramultiheadselfattenion_kernel(tc, table, w, delta, b_q, kv, b_v
         for jb in blocks:
             nc.vector.tensor_scalar_add(q_bf[jb][:], q_ps[jb][:], bq_sb[:, 0:1])
 
+        sc_bf_ps = [psum.tile([P, L], BF16, name=f"sc_bf_ps{jb}", tag=f"flip{jb}") for jb in blocks]
+        for jb in blocks:
+            nc.tensor.matmul(sc_bf_ps[jb][:], q_bf[jb][:], kv_sb[:], start=True, stop=True)
         sc_ps = [psum.tile([P, L], F32, name=f"sc_ps{jb}") for jb in blocks]
         for jb in blocks:
             nc.tensor.matmul(sc_ps[jb][:], q_bf[jb][:], kv_sb[:], start=True, stop=True)
 
-        neg_sc = [held.tile([P, L], F32, name=f"neg_sc{jb}") for jb in blocks]
+        neg_sc = [held.tile([P, L], BF16, name=f"neg_sc{jb}") for jb in blocks]
         shift = [held.tile([P, 1], F32, name=f"shift{jb}") for jb in blocks]
         e = [held.tile([P, L], F32, name=f"e{jb}") for jb in blocks]
         e_sum = [held.tile([P, 1], F32, name=f"e_sum{jb}") for jb in blocks]
         r_sum = [held.tile([P, 1], F32, name=f"r_sum{jb}") for jb in blocks]
         a = [held.tile([P, L], BF16, name=f"a{jb}") for jb in blocks]
         for jb in blocks:
-            nc.vector.tensor_scalar(neg_sc[jb][:], sc_ps[jb][:], -SCALE, None, op0=MULT, op1=MIN, accum_out=shift[jb][:])
-            nc.scalar.activation(e[jb][:], neg_sc[jb][:], EXP, bias=shift[jb][:, 0:1], scale=-1.0, accum_out=e_sum[jb][:])
+            nc.vector.tensor_scalar(neg_sc[jb][:], sc_bf_ps[jb][:], -SCALE, None, op0=MULT, op1=MIN, accum_out=shift[jb][:])
+            nc.scalar.activation(e[jb][:], sc_ps[jb][:], EXP, bias=shift[jb][:, 0:1], scale=SCALE, accum_out=e_sum[jb][:])
         a_t = [held.tile([P, L], BF16, name=f"a_t{jb}") for jb in blocks]
         o_ps = [psum.tile([P, P], F32, name=f"o_ps{jb}", tag=f"q_o{jb}") for jb in blocks]
         o = [held.tile([P, P], F32, name=f"o{jb}") for jb in blocks]

@@ -56,7 +56,7 @@ def tile_multiloramultiheadselfattenion_kernel(tc, table, w, delta, b_q, kv, b_v
 
         kv_t_ps = psum.tile([P, L], BF16, name="kv_t_ps", tag="flip2")
         for h in halves:
-            nc.tensor.transpose(kv_t_ps[:, h * P : (h + 1) * P], kv_sb[:, h * P : (h + 1) * P], identity[:])
+            nc.tensor.matmul(kv_t_ps[:, h * P : (h + 1) * P], kv_sb[:, h * P : (h + 1) * P], identity[:], start=True, stop=True)
         kv_t = held.tile([P, L], BF16, name="kv_t")
         nc.vector.tensor_copy(kv_t[:], kv_t_ps[:])
 
@@ -94,7 +94,7 @@ def tile_multiloramultiheadselfattenion_kernel(tc, table, w, delta, b_q, kv, b_v
                 keys = slice(h * P, (h + 1) * P)
                 nc.vector.tensor_scalar_mul(a[jb][:, keys], e[jb][:, keys], r_sum[jb][:, 0:1])
                 a_t_ps = psum.tile([P, P], BF16, name=f"a_t_ps{jb}{h}", tag=f"flip{2 * jb + h}")
-                nc.tensor.transpose(a_t_ps[:], a[jb][:, keys], identity[:])
+                nc.tensor.matmul(a_t_ps[:], a[jb][:, keys], identity[:], start=True, stop=True)
                 nc.vector.tensor_copy(a_t[jb][:, keys], a_t_ps[:])
                 nc.tensor.matmul(o_ps[jb][:], kv_t[:, keys], a_t[jb][:, keys], start=(h == 0), stop=(h == L // P - 1))
             nc.vector.tensor_scalar_add(o[jb][:], o_ps[jb][:], bv_sb[:, 0:1])

@@ -54,12 +54,6 @@ def tile_multiloramultiheadselfattenion_kernel(tc, table, w, delta, b_q, kv, b_v
             nc.tensor.transpose(table_t_ps[:], table_rows[:, b * P : (b + 1) * P], identity[:])
             nc.vector.tensor_copy(table_t[:, b * P : (b + 1) * P], table_t_ps[:])
 
-        kv_t_ps = psum.tile([P, L], BF16, name="kv_t_ps", tag="flip2")
-        for h in halves:
-            nc.tensor.matmul(kv_t_ps[:, h * P : (h + 1) * P], kv_sb[:, h * P : (h + 1) * P], identity[:], start=True, stop=True)
-        kv_t = held.tile([P, L], BF16, name="kv_t")
-        nc.vector.tensor_copy(kv_t[:], kv_t_ps[:])
-
         q_ps = [psum.tile([P, P], F32, name=f"q_ps{jb}", tag=f"q_o{jb}") for jb in blocks]
         q_bf = [held.tile([P, P], BF16, name=f"q_bf{jb}") for jb in blocks]
         for jb in blocks:
@@ -85,6 +79,12 @@ def tile_multiloramultiheadselfattenion_kernel(tc, table, w, delta, b_q, kv, b_v
         for jb in blocks:
             nc.vector.tensor_scalar(neg_sc[jb][:], sc_bf_ps[jb][:], -SCALE, None, op0=MULT, op1=MIN, accum_out=shift[jb][:])
             nc.scalar.activation(e[jb][:], sc_ps[jb][:], EXP, bias=shift[jb][:, 0:1], scale=SCALE, accum_out=e_sum[jb][:])
+        kv_t_ps = psum.tile([P, L], BF16, name="kv_t_ps", tag="q_o1")
+        for h in halves:
+            nc.tensor.matmul(kv_t_ps[:, h * P : (h + 1) * P], kv_sb[:, h * P : (h + 1) * P], identity[:], start=True, stop=True)
+        kv_t = held.tile([P, L], BF16, name="kv_t")
+        nc.scalar.copy(kv_t[:], kv_t_ps[:])
+
         a_t = [held.tile([P, L], BF16, name=f"a_t{jb}") for jb in blocks]
         o_ps = [psum.tile([P, P], F32, name=f"o_ps{jb}", tag=f"q_o{jb}") for jb in blocks]
         o = [held.tile([P, P], F32, name=f"o{jb}") for jb in blocks]

@@ -97,5 +97,7 @@ def tile_multiloramultiheadselfattenion_kernel(tc, table, w, delta, b_q, kv, b_v
                 nc.tensor.matmul(a_t_ps[:], a[jb][:, keys], identity[:], start=True, stop=True)
                 nc.vector.tensor_copy(a_t[jb][:, keys], a_t_ps[:])
                 nc.tensor.matmul(o_ps[jb][:], kv_t[:, keys], a_t[jb][:, keys], start=(h == 0), stop=(h == L // P - 1))
-            nc.vector.tensor_scalar_add(o[jb][:], o_ps[jb][:], bv_sb[:, 0:1])
-            nc.sync.dma_start(out[:, jb * P : (jb + 1) * P], o[jb][:])
+            for c, queue in enumerate((nc.sync, nc.scalar)):
+                cols = slice(c * (P // 2), (c + 1) * (P // 2))
+                nc.vector.tensor_scalar_add(o[jb][:, cols], o_ps[jb][:, cols], bv_sb[:, 0:1])
+                queue.dma_start(out[:, jb * P + c * (P // 2) : jb * P + (c + 1) * (P // 2)], o[jb][:, cols])

@@ -37,11 +37,13 @@ def tile_multiloramultiheadselfattenion_kernel(tc, table, w, delta, b_q, kv, b_v
         nc.scalar.dma_start(bq_sb[:], b_q)
         kv_sb = held.tile([P, L], BF16, name="kv_sb")
         nc.sync.dma_start(kv_sb[:], kv)
-        bv_sb = held.tile([P, 1], F32, name="bv_sb")
-        nc.scalar.dma_start(bv_sb[:], b_v)
+        bv_rows = held.tile([P, P], F32, name="bv_rows")
+        nc.scalar.dma_start(bv_rows[:], b_v.rearrange("m o -> (o m)").partition_broadcast(P))
 
         identity = held.tile([P, P], BF16, name="identity")
         make_identity(nc, identity[:])
+        identity_f32 = held.tile([P, P], F32, name="identity_f32")
+        nc.vector.tensor_copy(identity_f32[:], identity[:])
 
         scrap = held.tile([P, 1], F32, name="scrap")
         nc.vector.memset(scrap[:], 0.0)
@@ -53,6 +55,12 @@ def tile_multiloramultiheadselfattenion_kernel(tc, table, w, delta, b_q, kv, b_v
             table_t_ps = psum.tile([P, P], BF16, name=f"table_t_ps{b}", tag=f"flip{b}")
             nc.tensor.transpose(table_t_ps[:], table_rows[:, b * P : (b + 1) * P], identity[:])
             nc.vector.tensor_copy(table_t[:, b * P : (b + 1) * P], table_t_ps[:])
+
+        kv_t_ps = psum.tile([P, L], BF16, name="kv_t_ps", tag="flip2")
+        for h in halves:
+            nc.tensor.matmul(kv_t_ps[:, h * P : (h + 1) * P], kv_sb[:, h * P : (h + 1) * P], identity[:], start=True, stop=True)
+        kv_t = held.tile([P, L], BF16, name="kv_t")
+        nc.scalar.copy(kv_t[:], kv_t_ps[:])
 
         q_ps = [psum.tile([P, P], F32, name=f"q_ps{jb}", tag=f"q_o{jb}") for jb in blocks]
         q_bf = [held.tile([P, P], BF16, name=f"q_bf{jb}") for jb in blocks]
@@ -66,38 +74,40 @@ def tile_multiloramultiheadselfattenion_kernel(tc, table, w, delta, b_q, kv, b_v
         sc_bf_ps = [psum.tile([P, L], BF16, name=f"sc_bf_ps{jb}", tag=f"flip{jb}") for jb in blocks]
         for jb in blocks:
             nc.tensor.matmul(sc_bf_ps[jb][:], q_bf[jb][:], kv_sb[:], start=True, stop=True)
-        sc_ps = [psum.tile([P, L], F32, name=f"sc_ps{jb}") for jb in blocks]
+        sc_ps = [psum.tile([P, L], F32, name=f"sc_ps{jb}", tag=f"sc_ps{jb}") for jb in blocks]
         for jb in blocks:
             nc.tensor.matmul(sc_ps[jb][:], q_bf[jb][:], kv_sb[:], start=True, stop=True)
 
         neg_sc = [held.tile([P, L], BF16, name=f"neg_sc{jb}") for jb in blocks]
         shift = [held.tile([P, 1], F32, name=f"shift{jb}") for jb in blocks]
-        e = [held.tile([P, L], F32, name=f"e{jb}") for jb in blocks]
+        e = [held.tile([P, L], BF16, name=f"e{jb}") for jb in blocks]
         e_sum = [held.tile([P, 1], F32, name=f"e_sum{jb}") for jb in blocks]
         r_sum = [held.tile([P, 1], F32, name=f"r_sum{jb}") for jb in blocks]
-        a = [held.tile([P, L], BF16, name=f"a{jb}") for jb in blocks]
+        sum_bv = [held.tile([P, P], F32, name=f"sum_bv{jb}") for jb in blocks]
         for jb in blocks:
             nc.vector.tensor_scalar(neg_sc[jb][:], sc_bf_ps[jb][:], -SCALE, None, op0=MULT, op1=MIN, accum_out=shift[jb][:])
             nc.scalar.activation(e[jb][:], sc_ps[jb][:], EXP, bias=shift[jb][:, 0:1], scale=SCALE, accum_out=e_sum[jb][:])
-        kv_t_ps = psum.tile([P, L], BF16, name="kv_t_ps", tag="q_o1")
-        for h in halves:
-            nc.tensor.matmul(kv_t_ps[:, h * P : (h + 1) * P], kv_sb[:, h * P : (h + 1) * P], identity[:], start=True, stop=True)
-        kv_t = held.tile([P, L], BF16, name="kv_t")
-        nc.scalar.copy(kv_t[:], kv_t_ps[:])
-
-        a_t = [held.tile([P, L], BF16, name=f"a_t{jb}") for jb in blocks]
+            nc.vector.reciprocal(r_sum[jb][:], e_sum[jb][:])
+            nc.vector.tensor_scalar_mul(sum_bv[jb][:], bv_rows[:], e_sum[jb][:, 0:1])
+        rb = [held.tile([P, P], F32, name=f"rb{jb}") for jb in blocks]
+        e_t = [held.tile([P, L], BF16, name=f"e_t{jb}") for jb in blocks]
         o_ps = [psum.tile([P, P], F32, name=f"o_ps{jb}", tag=f"q_o{jb}") for jb in blocks]
         o = [held.tile([P, P], F32, name=f"o{jb}") for jb in blocks]
         for jb in blocks:
-            nc.vector.reciprocal(r_sum[jb][:], e_sum[jb][:])
             for h in halves:
                 keys = slice(h * P, (h + 1) * P)
-                nc.vector.tensor_scalar_mul(a[jb][:, keys], e[jb][:, keys], r_sum[jb][:, 0:1])
-                a_t_ps = psum.tile([P, P], BF16, name=f"a_t_ps{jb}{h}", tag=f"flip{2 * jb + h}")
-                nc.tensor.matmul(a_t_ps[:], a[jb][:, keys], identity[:], start=True, stop=True)
-                nc.vector.tensor_copy(a_t[jb][:, keys], a_t_ps[:])
-                nc.tensor.matmul(o_ps[jb][:], kv_t[:, keys], a_t[jb][:, keys], start=(h == 0), stop=(h == L // P - 1))
+                e_t_ps = psum.tile([P, P], BF16, name=f"e_t_ps{jb}{h}", tag=f"flip{2 * jb + h}")
+                nc.tensor.matmul(e_t_ps[:], e[jb][:, keys], identity[:], start=True, stop=True)
+                nc.vector.tensor_copy(e_t[jb][:, keys], e_t_ps[:])
+            rb_ps = psum.tile([P, P], F32, name=f"rb_ps{jb}", tag=f"sc_ps{jb}")
+            nc.tensor.transpose(rb_ps[:], r_sum[jb][:].to_broadcast([P, P]), identity_f32[:])
+            nc.scalar.copy(rb[jb][:], rb_ps[:])
+            nc.tensor.matmul(o_ps[jb][:], sum_bv[jb][:], identity_f32[:], start=True, stop=False)
+        for jb in blocks:
+            for h in halves:
+                keys = slice(h * P, (h + 1) * P)
+                nc.tensor.matmul(o_ps[jb][:], kv_t[:, keys], e_t[jb][:, keys], start=False, stop=(h == L // P - 1))
             for c, queue in enumerate((nc.sync, nc.scalar)):
                 cols = slice(c * (P // 2), (c + 1) * (P // 2))
-                nc.vector.tensor_scalar_add(o[jb][:, cols], o_ps[jb][:, cols], bv_sb[:, 0:1])
+                nc.vector.tensor_tensor(o[jb][:, cols], o_ps[jb][:, cols], rb[jb][:, cols], MULT)
                 queue.dma_start(out[:, jb * P + c * (P // 2) : jb * P + (c + 1) * (P // 2)], o[jb][:, cols])

@@ -37,8 +37,8 @@ def tile_multiloramultiheadselfattenion_kernel(tc, table, w, delta, b_q, kv, b_v
         nc.scalar.dma_start(bq_sb[:], b_q)
         kv_sb = held.tile([P, L], BF16, name="kv_sb")
         nc.sync.dma_start(kv_sb[:], kv)
-        bv_rows = held.tile([P, P], F32, name="bv_rows")
-        nc.scalar.dma_start(bv_rows[:], b_v.rearrange("m o -> (o m)").partition_broadcast(P))
+        bv_sb = held.tile([P, 1], F32, name="bv_sb")
+        nc.scalar.dma_start(bv_sb[:], b_v)
 
         identity = held.tile([P, P], BF16, name="identity")
         make_identity(nc, identity[:])
@@ -83,15 +83,14 @@ def tile_multiloramultiheadselfattenion_kernel(tc, table, w, delta, b_q, kv, b_v
         e = [held.tile([P, L], BF16, name=f"e{jb}") for jb in blocks]
         e_sum = [held.tile([P, 1], F32, name=f"e_sum{jb}") for jb in blocks]
         r_sum = [held.tile([P, 1], F32, name=f"r_sum{jb}") for jb in blocks]
-        sum_bv = [held.tile([P, P], F32, name=f"sum_bv{jb}") for jb in blocks]
         for jb in blocks:
             nc.vector.tensor_scalar(neg_sc[jb][:], sc_bf_ps[jb][:], -SCALE, None, op0=MULT, op1=MIN, accum_out=shift[jb][:])
             nc.scalar.activation(e[jb][:], sc_ps[jb][:], EXP, bias=shift[jb][:, 0:1], scale=SCALE, accum_out=e_sum[jb][:])
             nc.vector.reciprocal(r_sum[jb][:], e_sum[jb][:])
-            nc.vector.tensor_scalar_mul(sum_bv[jb][:], bv_rows[:], e_sum[jb][:, 0:1])
         rb = [held.tile([P, P], F32, name=f"rb{jb}") for jb in blocks]
         e_t = [held.tile([P, L], BF16, name=f"e_t{jb}") for jb in blocks]
         o_ps = [psum.tile([P, P], F32, name=f"o_ps{jb}", tag=f"q_o{jb}") for jb in blocks]
+        scaled = [held.tile([P, P], F32, name=f"scaled{jb}") for jb in blocks]
         o = [held.tile([P, P], F32, name=f"o{jb}") for jb in blocks]
         for jb in blocks:
             for h in halves:
@@ -99,15 +98,15 @@ def tile_multiloramultiheadselfattenion_kernel(tc, table, w, delta, b_q, kv, b_v
                 e_t_ps = psum.tile([P, P], BF16, name=f"e_t_ps{jb}{h}", tag=f"flip{2 * jb + h}")
                 nc.tensor.matmul(e_t_ps[:], e[jb][:, keys], identity[:], start=True, stop=True)
                 nc.vector.tensor_copy(e_t[jb][:, keys], e_t_ps[:])
+        for jb in blocks:
             rb_ps = psum.tile([P, P], F32, name=f"rb_ps{jb}", tag=f"sc_ps{jb}")
             nc.tensor.transpose(rb_ps[:], r_sum[jb][:].to_broadcast([P, P]), identity_f32[:])
             nc.scalar.copy(rb[jb][:], rb_ps[:])
-            nc.tensor.matmul(o_ps[jb][:], sum_bv[jb][:], identity_f32[:], start=True, stop=False)
-        for jb in blocks:
             for h in halves:
                 keys = slice(h * P, (h + 1) * P)
-                nc.tensor.matmul(o_ps[jb][:], kv_t[:, keys], e_t[jb][:, keys], start=False, stop=(h == L // P - 1))
+                nc.tensor.matmul(o_ps[jb][:], kv_t[:, keys], e_t[jb][:, keys], start=(h == 0), stop=(h == L // P - 1))
             for c, queue in enumerate((nc.sync, nc.scalar)):
                 cols = slice(c * (P // 2), (c + 1) * (P // 2))
-                nc.vector.tensor_tensor(o[jb][:, cols], o_ps[jb][:, cols], rb[jb][:, cols], MULT)
+                nc.vector.tensor_tensor(scaled[jb][:, cols], o_ps[jb][:, cols], rb[jb][:, cols], MULT)
+                nc.vector.tensor_scalar_add(o[jb][:, cols], scaled[jb][:, cols], bv_sb[:, 0:1])
                 queue.dma_start(out[:, jb * P + c * (P // 2) : jb * P + (c + 1) * (P // 2)], o[jb][:, cols])

@@ -33,10 +33,10 @@ def tile_multiloramultiheadselfattenion_kernel(tc, table, w, delta, b_q, kv, b_v
         nc.scalar.dma_start(delta_sb[:], delta)
         w_sb = held.tile([P, P], BF16, name="w_sb")
         nc.sync.dma_start(w_sb[:], w)
-        bq_sb = held.tile([P, 1], F32, name="bq_sb")
-        nc.scalar.dma_start(bq_sb[:], b_q)
         kv_sb = held.tile([P, L], BF16, name="kv_sb")
-        nc.sync.dma_start(kv_sb[:], kv)
+        nc.scalar.dma_start(kv_sb[:], kv)
+        bq_sb = held.tile([P, 1], F32, name="bq_sb")
+        nc.sync.dma_start(bq_sb[:], b_q)
         bv_sb = held.tile([P, 1], F32, name="bv_sb")
         nc.scalar.dma_start(bv_sb[:], b_v)
 

@@ -89,7 +89,6 @@ def tile_multiloramultiheadselfattenion_kernel(tc, table, w, delta, b_q, kv, b_v
             nc.vector.reciprocal(r_sum[jb][:], e_sum[jb][:])
         rb = [held.tile([P, P], F32, name=f"rb{jb}") for jb in blocks]
         e_t = [held.tile([P, L], BF16, name=f"e_t{jb}") for jb in blocks]
-        o_ps = [psum.tile([P, P], F32, name=f"o_ps{jb}", tag=f"q_o{jb}") for jb in blocks]
         scaled = [held.tile([P, P], F32, name=f"scaled{jb}") for jb in blocks]
         o = [held.tile([P, P], F32, name=f"o{jb}") for jb in blocks]
         for jb in blocks:
@@ -102,11 +101,12 @@ def tile_multiloramultiheadselfattenion_kernel(tc, table, w, delta, b_q, kv, b_v
             rb_ps = psum.tile([P, P], F32, name=f"rb_ps{jb}", tag=f"sc_ps{jb}")
             nc.tensor.transpose(rb_ps[:], r_sum[jb][:].to_broadcast([P, P]), identity_f32[:])
             nc.scalar.copy(rb[jb][:], rb_ps[:])
-            for h in halves:
-                keys = slice(h * P, (h + 1) * P)
-                nc.tensor.matmul(o_ps[jb][:], kv_t[:, keys], e_t[jb][:, keys], start=(h == 0), stop=(h == L // P - 1))
+            o_ps = [psum.tile([P, P // 2], F32, name=f"o_ps{jb}{c}", tag=f"{bank}{jb}") for c, bank in enumerate(("q_o", "flip"))]
             for c, queue in enumerate((nc.sync, nc.scalar)):
                 cols = slice(c * (P // 2), (c + 1) * (P // 2))
-                nc.vector.tensor_tensor(scaled[jb][:, cols], o_ps[jb][:, cols], rb[jb][:, cols], MULT)
+                for h in halves:
+                    queries = slice(h * P + c * (P // 2), h * P + (c + 1) * (P // 2))
+                    nc.tensor.matmul(o_ps[c][:], kv_t[:, h * P : (h + 1) * P], e_t[jb][:, queries], start=(h == 0), stop=(h == L // P - 1))
+                nc.vector.tensor_tensor(scaled[jb][:, cols], o_ps[c][:], rb[jb][:, cols], MULT)
                 nc.vector.tensor_scalar_add(o[jb][:, cols], scaled[jb][:, cols], bv_sb[:, 0:1])
                 queue.dma_start(out[:, jb * P + c * (P // 2) : jb * P + (c + 1) * (P // 2)], o[jb][:, cols])

import math

import concourse.mybir as mybir
from concourse.masks import make_identity

BF16, F32, U16 = mybir.dt.bfloat16, mybir.dt.float32, mybir.dt.uint16
EXP = mybir.ActivationFunctionType.Exp
MULT, MIN = mybir.AluOpType.mult, mybir.AluOpType.min

P = 128
S = 256
N = 256
L = 256
SCALE = 1.0 / math.sqrt(P)

FLOPS = 2 * (2 * P * P * N) + 2 * (2 * P * N * L)


def tile_multiloramultiheadselfattenion_kernel(tc, table, w, delta, b_q, kv, b_v, offs, out):
    nc = tc.nc
    blocks = range(N // P)
    halves = range(L // P)
    with (
        tc.tile_pool(name="held", bufs=1) as held,
        tc.psum_pool(name="psum", bufs=1) as psum,
    ):
        table_rows = held.tile([P, S], BF16, name="table_rows")
        nc.sync.dma_start(table_rows[:, 0:P], table[0:P, :])
        nc.scalar.dma_start(table_rows[:, P : 2 * P], table[P : 2 * P, :])
        offsets = held.tile([P, N // 16], U16, name="offsets")
        nc.sync.dma_start(offsets[:], offs)
        delta_sb = held.tile([P, P], BF16, name="delta_sb")
        nc.scalar.dma_start(delta_sb[:], delta)
        w_sb = held.tile([P, P], BF16, name="w_sb")
        nc.sync.dma_start(w_sb[:], w)
        kv_sb = held.tile([P, L], BF16, name="kv_sb")
        nc.scalar.dma_start(kv_sb[:], kv)
        bq_sb = held.tile([P, 1], F32, name="bq_sb")
        nc.sync.dma_start(bq_sb[:], b_q)
        bv_sb = held.tile([P, 1], F32, name="bv_sb")
        nc.scalar.dma_start(bv_sb[:], b_v)

        identity = held.tile([P, P], BF16, name="identity")
        make_identity(nc, identity[:])
        identity_f32 = held.tile([P, P], F32, name="identity_f32")
        nc.vector.tensor_copy(identity_f32[:], identity[:])

        scrap = held.tile([P, 1], F32, name="scrap")
        nc.vector.memset(scrap[:], 0.0)
        scrap_exp = held.tile([P, 1], F32, name="scrap_exp")
        nc.scalar.activation(scrap_exp[:], scrap[:], EXP)

        table_t = held.tile([P, S], BF16, name="table_t")
        for b in range(S // P):
            table_t_ps = psum.tile([P, P], BF16, name=f"table_t_ps{b}", tag=f"flip{b}")
            nc.tensor.transpose(table_t_ps[:], table_rows[:, b * P : (b + 1) * P], identity[:])
            nc.vector.tensor_copy(table_t[:, b * P : (b + 1) * P], table_t_ps[:])

        kv_t_ps = psum.tile([P, L], BF16, name="kv_t_ps", tag="flip2")
        for h in halves:
            nc.tensor.matmul(kv_t_ps[:, h * P : (h + 1) * P], kv_sb[:, h * P : (h + 1) * P], identity[:], start=True, stop=True)
        kv_t = held.tile([P, L], BF16, name="kv_t")
        nc.scalar.copy(kv_t[:], kv_t_ps[:])

        q_ps = [psum.tile([P, P], F32, name=f"q_ps{jb}", tag=f"q_o{jb}") for jb in blocks]
        q_bf = [held.tile([P, P], BF16, name=f"q_bf{jb}") for jb in blocks]
        for jb in blocks:
            piece = offsets[:, jb * (P // 16) : (jb + 1) * (P // 16)]
            nc.tensor.matmul(q_ps[jb][:], w_sb[:], table_t[:].indirect(piece), start=True, stop=False)
            nc.tensor.matmul(q_ps[jb][:], delta_sb[:], table_t[:].indirect(piece), start=False, stop=True)
        for jb in blocks:
            nc.vector.tensor_scalar_add(q_bf[jb][:], q_ps[jb][:], bq_sb[:, 0:1])

        sc_bf_ps = [psum.tile([P, L], BF16, name=f"sc_bf_ps{jb}", tag=f"flip{jb}") for jb in blocks]
        for jb in blocks:
            nc.tensor.matmul(sc_bf_ps[jb][:], q_bf[jb][:], kv_sb[:], start=True, stop=True)
        sc_ps = [psum.tile([P, L], F32, name=f"sc_ps{jb}", tag=f"sc_ps{jb}") for jb in blocks]
        for jb in blocks:
            nc.tensor.matmul(sc_ps[jb][:], q_bf[jb][:], kv_sb[:], start=True, stop=True)

        neg_sc = [held.tile([P, L], BF16, name=f"neg_sc{jb}") for jb in blocks]
        shift = [held.tile([P, 1], F32, name=f"shift{jb}") for jb in blocks]
        e = [held.tile([P, L], BF16, name=f"e{jb}") for jb in blocks]
        e_sum = [held.tile([P, 1], F32, name=f"e_sum{jb}") for jb in blocks]
        r_sum = [held.tile([P, 1], F32, name=f"r_sum{jb}") for jb in blocks]
        for jb in blocks:
            nc.vector.tensor_scalar(neg_sc[jb][:], sc_bf_ps[jb][:], -SCALE, None, op0=MULT, op1=MIN, accum_out=shift[jb][:])
            nc.scalar.activation(e[jb][:], sc_ps[jb][:], EXP, bias=shift[jb][:, 0:1], scale=SCALE, accum_out=e_sum[jb][:])
            nc.vector.reciprocal(r_sum[jb][:], e_sum[jb][:])
        rb = [held.tile([P, P], F32, name=f"rb{jb}") for jb in blocks]
        e_t = [held.tile([P, L], BF16, name=f"e_t{jb}") for jb in blocks]
        scaled = [held.tile([P, P], F32, name=f"scaled{jb}") for jb in blocks]
        o = [held.tile([P, P], F32, name=f"o{jb}") for jb in blocks]
        for jb in blocks:
            for h in halves:
                keys = slice(h * P, (h + 1) * P)
                e_t_ps = psum.tile([P, P], BF16, name=f"e_t_ps{jb}{h}", tag=f"flip{2 * jb + h}")
                nc.tensor.matmul(e_t_ps[:], e[jb][:, keys], identity[:], start=True, stop=True)
                nc.vector.tensor_copy(e_t[jb][:, keys], e_t_ps[:])
        for jb in blocks:
            rb_ps = psum.tile([P, P], F32, name=f"rb_ps{jb}", tag=f"sc_ps{jb}")
            nc.tensor.transpose(rb_ps[:], r_sum[jb][:].to_broadcast([P, P]), identity_f32[:])
            nc.scalar.copy(rb[jb][:], rb_ps[:])
            o_ps = [psum.tile([P, P // 2], F32, name=f"o_ps{jb}{c}", tag=f"{bank}{jb}") for c, bank in enumerate(("q_o", "flip"))]
            for c, queue in enumerate((nc.sync, nc.scalar)):
                cols = slice(c * (P // 2), (c + 1) * (P // 2))
                for h in halves:
                    queries = slice(h * P + c * (P // 2), h * P + (c + 1) * (P // 2))
                    nc.tensor.matmul(o_ps[c][:], kv_t[:, h * P : (h + 1) * P], e_t[jb][:, queries], start=(h == 0), stop=(h == L // P - 1))
                nc.vector.tensor_tensor(scaled[jb][:, cols], o_ps[c][:], rb[jb][:, cols], MULT)
                nc.vector.tensor_scalar_add(o[jb][:, cols], scaled[jb][:, cols], bv_sb[:, 0:1])
                queue.dma_start(out[:, jb * P + c * (P // 2) : jb * P + (c + 1) * (P // 2)], o[jb][:, cols])
